import numpy as np
import ml_dtypes


def mxq(x, axis, fmt="e4m3"):
    dtype, down = {"e4m3": (ml_dtypes.float8_e4m3fn, 7), "e5m2": (ml_dtypes.float8_e5m2, 14)}[fmt]
    v = np.moveaxis(np.asarray(x, np.float32).astype(ml_dtypes.bfloat16).astype(np.float64), axis, -1)
    blocks = v.reshape(v.shape[:-1] + (-1, 32))
    amax = np.abs(blocks).max(-1, keepdims=True)
    byte = np.maximum(np.where(amax > 0, np.frexp(amax)[1] - 1 + 127, 0) - down, 1)
    scale = np.exp2(byte - 127.0)
    codes = (blocks / scale).astype(np.float32).astype(dtype).astype(np.float64)
    return np.moveaxis((codes * scale).reshape(v.shape), -1, axis)


WIDE = False


def mx_kscale(k):
    if not WIDE:
        return np.ones(k)
    levels = np.array([10, -10, 5, -5, 0])
    a = np.random.permutation(np.resize(levels, k // 512 * 4)).reshape(k // 512, 4)
    idx = np.arange(k)
    return np.exp2(a[idx // 512, idx % 128 // 32])


BF16 = ml_dtypes.bfloat16


def bf(x):
    return np.asarray(x, np.float32).astype(BF16)


def f64(x):
    return np.asarray(x).astype(np.float64)


B, S, K, N = 4, 2048, 1024, 128
THRESHOLD = 0.3


def ternary_quantize(w, threshold=THRESHOLD):
    return np.sign(w) * (np.abs(w) > threshold)


def ternary_ste(w, threshold=THRESHOLD):
    return w + (ternary_quantize(w, threshold) - w)


def setup_inputs():
    s = mx_kscale(K)
    r = s / s.min()
    return {"x": bf(np.random.standard_normal((B, S, K)) * 8.0 / np.sqrt(K) * r),
            "kernel": bf(0.2 * np.random.standard_normal((K, N)) / r[:, None])}


def reference(x, kernel):
    w_ternary = ternary_ste(f64(kernel), THRESHOLD)
    return mxq(f64(x), 2, "e4m3") @ mxq(w_ternary, 0, "e4m3")

@@ -1,0 +1,146 @@
+from contextlib import ExitStack
+
+import concourse.masks as masks
+import concourse.mybir as mybir
+
+F32 = mybir.dt.float32
+BF16 = mybir.dt.bfloat16
+U32 = mybir.dt.uint32
+U8 = mybir.dt.uint8
+FP8X4 = mybir.dt.float8_e4m3fn_x4
+ALU = mybir.AluOpType
+
+P = 128
+ROWS = 8192
+K = 1024
+N = 128
+NT = ROWS // P
+RUN = 4
+QT = 2
+NCH = NT // RUN
+THRESHOLD = 0.3
+FLOPS = 2 * ROWS * K * N
+
+LOAD_PLAN = [2, 2] + [4] * 15
+STORE_PLAN = [4, 4, 4, 2, 1, 1]
+VECTOR_BANK = 1
+
+
+def tile_ternarylinear_t_kernel(tc, x, kernel, out):
+    nc = tc.nc
+    xv = x.flatten_outer_dims().rearrange("(p t) k -> p (t k)", t=NT)
+    ov = out.flatten_outer_dims().rearrange("(p t) n -> p (t n)", t=NT)
+
+    with ExitStack() as ctx:
+        xpool = ctx.enter_context(tc.tile_pool(name="xpool", bufs=1))
+        wk = ctx.enter_context(tc.tile_pool(name="wk", bufs=1))
+        opool = ctx.enter_context(tc.tile_pool(name="opool", bufs=1))
+        stage = ctx.enter_context(tc.tile_pool(name="stage", bufs=6))
+        tps = ctx.enter_context(tc.psum_pool(name="tps", bufs=6))
+        ops = ctx.enter_context(tc.psum_pool(name="ops", bufs=2))
+        ctx.enter_context(tc.manual_schedule())
+
+        k_sb = wk.tile([P, 8 * N], BF16, name="k_sb")
+        nc.scalar.dma_start(
+            out=k_sb[:].rearrange("q (a f) -> q a f", a=4),
+            in_=kernel.rearrange("(a q e) n -> q a (e n)", a=4, q=P, e=2),
+        )
+        x_words = []
+        t0 = 0
+        for l, cnt in enumerate(LOAD_PLAN):
+            xt = xpool.tile([P, cnt * K], BF16, name="x%d" % l)
+            nc.sync.dma_start(out=xt[:], in_=xv[:, t0 * K : (t0 + cnt) * K])
+            words = xt[:].bitcast(F32)
+            for i in range(cnt):
+                x_words.append(words[:, i * (K // 2) : (i + 1) * (K // 2)])
+            t0 += cnt
+
+        ident = wk.tile([P, P], F32, name="ident")
+        masks.make_identity(nc, ident[:])
+
+        pos = wk.tile([P, 8 * N], BF16, name="pos")
+        neg = wk.tile([P, 8 * N], BF16, name="neg")
+        nc.vector.tensor_scalar(out=pos[:], in0=k_sb[:], scalar1=THRESHOLD, scalar2=None, op0=ALU.is_gt)
+        nc.vector.tensor_scalar(out=neg[:], in0=k_sb[:], scalar1=-THRESHOLD, scalar2=None, op0=ALU.is_lt)
+        w_bf = wk.tile([P, 8 * N], BF16, name="w_bf", align_bytes=64)
+        nc.vector.tensor_tensor(
+            out=w_bf[:].rearrange("q (g n t) -> q g n t", g=2, n=N, t=4),
+            in0=pos[:].rearrange("q (g t n) -> q g n t", g=2, n=N, t=4),
+            in1=neg[:].rearrange("q (g t n) -> q g n t", g=2, n=N, t=4),
+            op=ALU.subtract,
+        )
+        w_codes = wk.tile([P, 2 * N], U32, name="w_codes", align_bytes=64)
+        w_scales = wk.tile([P, 2 * N], U8, name="w_scales", align_bytes=64)
+        nc.vector.quantize_mx(out=w_codes[:].bitcast(FP8X4), scales=w_scales[:], in_=w_bf[:])
+
+        out_slices = []
+        c0 = 0
+        for s, cnt in enumerate(STORE_PLAN):
+            ot = opool.tile([P, cnt * RUN * N], F32, name="o%d" % s)
+            for i in range(cnt):
+                last = i == cnt - 1
+                out_slices.append((ot[:, i * RUN * N : (i + 1) * RUN * N], (ot, c0, cnt) if last else None))
+            c0 += cnt
+
+        banks = {}
+        quantised = {}
+
+        def transposes(c):
+            for i in range(RUN):
+                bank = tps.tile([P, 512], F32, name="tb")
+                banks[(c, i)] = bank
+                for j in range(4):
+                    nc.tensor.transpose(bank[:, j * P : (j + 1) * P], x_words[c * RUN + i][:, j * P : (j + 1) * P], ident[:])
+
+        def copies_and_quantise(c):
+            groups = []
+            for h in range(RUN // QT):
+                grp = stage.tile([P, QT * K], BF16, name="grp", align_bytes=64)
+                groups.append(grp)
+            for i in range(RUN):
+                grp = groups[i // QT]
+                dst = grp[:].bitcast(F32)[:, (i % QT) * 512 : (i % QT + 1) * 512].rearrange(
+                    "p (g r u) -> p g r u", g=2, r=P, u=2
+                )
+                src = banks[(c, i)][:].rearrange("p (g u r) -> p g r u", g=2, u=2, r=P)
+                if i == VECTOR_BANK:
+                    nc.vector.tensor_copy(out=dst, in_=src)
+                else:
+                    nc.scalar.copy(out=dst, in_=src)
+            for h in range(RUN // QT):
+                codes = stage.tile([P, QT * K // 4], U32, name="codes", align_bytes=64)
+                scales = stage.tile([P, QT * K // 4], U8, name="scales", align_bytes=64)
+                nc.vector.quantize_mx(out=codes[:].bitcast(FP8X4), scales=scales[:], in_=groups[h][:])
+                quantised[(c, h)] = (codes, scales)
+
+        def multiply(c):
+            acc = ops.tile([P, RUN * N], F32, name="acc")
+            for i in range(RUN):
+                codes, scales = quantised[(c, i // QT)]
+                for g in range(2):
+                    lo = ((i % QT) * 2 + g) * P
+                    nc.tensor.matmul_mx(
+                        out=acc[:, i * N : (i + 1) * N],
+                        lhsT=codes[:, lo : lo + P].bitcast(FP8X4),
+                        lhsT_scale=scales[:, lo : lo + P],
+                        rhs=w_codes[:, g * N : (g + 1) * N].bitcast(FP8X4),
+                        rhs_scale=w_scales[:, g * N : (g + 1) * N],
+                        start=(g == 0),
+                        stop=(g == 1),
+                    )
+            dst, store = out_slices[c]
+            if c % 2 == 0:
+                nc.vector.tensor_copy(out=dst, in_=acc[:])
+            else:
+                nc.scalar.copy(out=dst, in_=acc[:])
+            if store is not None:
+                ot, first, cnt = store
+                nc.sync.dma_start(out=ov[:, first * RUN * N : (first + cnt) * RUN * N], in_=ot[:])
+
+        transposes(0)
+        copies_and_quantise(0)
+        for c in range(NCH):
+            if c + 1 < NCH:
+                transposes(c + 1)
+                copies_and_quantise(c + 1)
+            multiply(c)

@@ -21,8 +21,8 @@ NCH = NT // RUN
 THRESHOLD = 0.3
 FLOPS = 2 * ROWS * K * N
 
-LOAD_PLAN = [2, 2] + [4] * 15
-STORE_PLAN = [4, 4, 4, 2, 1, 1]
+LOAD_PLAN = [2, 2, 4] + [8] * 6 + [4, 4]
+STORE_PLAN = [8, 4, 2, 1, 1]
 VECTOR_BANK = 1
 
 

@@ -21,8 +21,8 @@ NCH = NT // RUN
 THRESHOLD = 0.3
 FLOPS = 2 * ROWS * K * N
 
-LOAD_PLAN = [2, 2, 4] + [8] * 6 + [4, 4]
-STORE_PLAN = [8, 4, 2, 1, 1]
+LOAD_PLAN = [2, 2] + [4] * 15
+STORE_PLAN = [4, 4, 4, 2, 1, 1]
 VECTOR_BANK = 1
 
 
@@ -92,7 +92,9 @@ def tile_ternarylinear_t_kernel(tc, x, kernel, out):
                 for j in range(4):
                     nc.tensor.transpose(bank[:, j * P : (j + 1) * P], x_words[c * RUN + i][:, j * P : (j + 1) * P], ident[:])
 
-        def copies_and_quantise(c):
+        grouped = {}
+
+        def copies(c):
             groups = []
             for h in range(RUN // QT):
                 grp = stage.tile([P, QT * K], BF16, name="grp", align_bytes=64)
@@ -107,6 +109,10 @@ def tile_ternarylinear_t_kernel(tc, x, kernel, out):
                     nc.vector.tensor_copy(out=dst, in_=src)
                 else:
                     nc.scalar.copy(out=dst, in_=src)
+            grouped[c] = groups
+
+        def quantise(c):
+            groups = grouped[c]
             for h in range(RUN // QT):
                 codes = stage.tile([P, QT * K // 4], U32, name="codes", align_bytes=64)
                 scales = stage.tile([P, QT * K // 4], U8, name="scales", align_bytes=64)
@@ -137,10 +143,11 @@ def tile_ternarylinear_t_kernel(tc, x, kernel, out):
                 ot, first, cnt = store
                 nc.sync.dma_start(out=ov[:, first * RUN * N : (first + cnt) * RUN * N], in_=ot[:])
 
-        transposes(0)
-        copies_and_quantise(0)
-        for c in range(NCH):
-            if c + 1 < NCH:
-                transposes(c + 1)
-                copies_and_quantise(c + 1)
-            multiply(c)
+        for step in range(NCH + 2):
+            if step < NCH:
+                transposes(step)
+                copies(step)
+            if 0 <= step - 1 < NCH:
+                quantise(step - 1)
+            if step - 2 >= 0:
+                multiply(step - 2)

@@ -22,7 +22,7 @@ THRESHOLD = 0.3
 FLOPS = 2 * ROWS * K * N
 
 LOAD_PLAN = [2, 2] + [4] * 15
-STORE_PLAN = [4, 4, 4, 2, 1, 1]
+STORE_PLAN = [10, 4, 2]
 VECTOR_BANK = 1
 
 

from contextlib import ExitStack

import concourse.masks as masks
import concourse.mybir as mybir

F32 = mybir.dt.float32
BF16 = mybir.dt.bfloat16
U32 = mybir.dt.uint32
U8 = mybir.dt.uint8
FP8X4 = mybir.dt.float8_e4m3fn_x4
ALU = mybir.AluOpType

P = 128
ROWS = 8192
K = 1024
N = 128
NT = ROWS // P
RUN = 4
QT = 2
NCH = NT // RUN
THRESHOLD = 0.3
FLOPS = 2 * ROWS * K * N

LOAD_PLAN = [2, 2] + [4] * 15
STORE_PLAN = [10, 4, 2]
VECTOR_BANK = 1


def tile_ternarylinear_t_kernel(tc, x, kernel, out):
    nc = tc.nc
    xv = x.flatten_outer_dims().rearrange("(p t) k -> p (t k)", t=NT)
    ov = out.flatten_outer_dims().rearrange("(p t) n -> p (t n)", t=NT)

    with ExitStack() as ctx:
        xpool = ctx.enter_context(tc.tile_pool(name="xpool", bufs=1))
        wk = ctx.enter_context(tc.tile_pool(name="wk", bufs=1))
        opool = ctx.enter_context(tc.tile_pool(name="opool", bufs=1))
        stage = ctx.enter_context(tc.tile_pool(name="stage", bufs=6))
        tps = ctx.enter_context(tc.psum_pool(name="tps", bufs=6))
        ops = ctx.enter_context(tc.psum_pool(name="ops", bufs=2))
        ctx.enter_context(tc.manual_schedule())

        k_sb = wk.tile([P, 8 * N], BF16, name="k_sb")
        nc.scalar.dma_start(
            out=k_sb[:].rearrange("q (a f) -> q a f", a=4),
            in_=kernel.rearrange("(a q e) n -> q a (e n)", a=4, q=P, e=2),
        )
        x_words = []
        t0 = 0
        for l, cnt in enumerate(LOAD_PLAN):
            xt = xpool.tile([P, cnt * K], BF16, name="x%d" % l)
            nc.sync.dma_start(out=xt[:], in_=xv[:, t0 * K : (t0 + cnt) * K])
            words = xt[:].bitcast(F32)
            for i in range(cnt):
                x_words.append(words[:, i * (K // 2) : (i + 1) * (K // 2)])
            t0 += cnt

        ident = wk.tile([P, P], F32, name="ident")
        masks.make_identity(nc, ident[:])

        pos = wk.tile([P, 8 * N], BF16, name="pos")
        neg = wk.tile([P, 8 * N], BF16, name="neg")
        nc.vector.tensor_scalar(out=pos[:], in0=k_sb[:], scalar1=THRESHOLD, scalar2=None, op0=ALU.is_gt)
        nc.vector.tensor_scalar(out=neg[:], in0=k_sb[:], scalar1=-THRESHOLD, scalar2=None, op0=ALU.is_lt)
        w_bf = wk.tile([P, 8 * N], BF16, name="w_bf", align_bytes=64)
        nc.vector.tensor_tensor(
            out=w_bf[:].rearrange("q (g n t) -> q g n t", g=2, n=N, t=4),
            in0=pos[:].rearrange("q (g t n) -> q g n t", g=2, n=N, t=4),
            in1=neg[:].rearrange("q (g t n) -> q g n t", g=2, n=N, t=4),
            op=ALU.subtract,
        )
        w_codes = wk.tile([P, 2 * N], U32, name="w_codes", align_bytes=64)
        w_scales = wk.tile([P, 2 * N], U8, name="w_scales", align_bytes=64)
        nc.vector.quantize_mx(out=w_codes[:].bitcast(FP8X4), scales=w_scales[:], in_=w_bf[:])

        out_slices = []
        c0 = 0
        for s, cnt in enumerate(STORE_PLAN):
            ot = opool.tile([P, cnt * RUN * N], F32, name="o%d" % s)
            for i in range(cnt):
                last = i == cnt - 1
                out_slices.append((ot[:, i * RUN * N : (i + 1) * RUN * N], (ot, c0, cnt) if last else None))
            c0 += cnt

        banks = {}
        quantised = {}

        def transposes(c):
            for i in range(RUN):
                bank = tps.tile([P, 512], F32, name="tb")
                banks[(c, i)] = bank
                for j in range(4):
                    nc.tensor.transpose(bank[:, j * P : (j + 1) * P], x_words[c * RUN + i][:, j * P : (j + 1) * P], ident[:])

        grouped = {}

        def copies(c):
            groups = []
            for h in range(RUN // QT):
                grp = stage.tile([P, QT * K], BF16, name="grp", align_bytes=64)
                groups.append(grp)
            for i in range(RUN):
                grp = groups[i // QT]
                dst = grp[:].bitcast(F32)[:, (i % QT) * 512 : (i % QT + 1) * 512].rearrange(
                    "p (g r u) -> p g r u", g=2, r=P, u=2
                )
                src = banks[(c, i)][:].rearrange("p (g u r) -> p g r u", g=2, u=2, r=P)
                if i == VECTOR_BANK:
                    nc.vector.tensor_copy(out=dst, in_=src)
                else:
                    nc.scalar.copy(out=dst, in_=src)
            grouped[c] = groups

        def quantise(c):
            groups = grouped[c]
            for h in range(RUN // QT):
                codes = stage.tile([P, QT * K // 4], U32, name="codes", align_bytes=64)
                scales = stage.tile([P, QT * K // 4], U8, name="scales", align_bytes=64)
                nc.vector.quantize_mx(out=codes[:].bitcast(FP8X4), scales=scales[:], in_=groups[h][:])
                quantised[(c, h)] = (codes, scales)

        def multiply(c):
            acc = ops.tile([P, RUN * N], F32, name="acc")
            for i in range(RUN):
                codes, scales = quantised[(c, i // QT)]
                for g in range(2):
                    lo = ((i % QT) * 2 + g) * P
                    nc.tensor.matmul_mx(
                        out=acc[:, i * N : (i + 1) * N],
                        lhsT=codes[:, lo : lo + P].bitcast(FP8X4),
                        lhsT_scale=scales[:, lo : lo + P],
                        rhs=w_codes[:, g * N : (g + 1) * N].bitcast(FP8X4),
                        rhs_scale=w_scales[:, g * N : (g + 1) * N],
                        start=(g == 0),
                        stop=(g == 1),
                    )
            dst, store = out_slices[c]
            if c % 2 == 0:
                nc.vector.tensor_copy(out=dst, in_=acc[:])
            else:
                nc.scalar.copy(out=dst, in_=acc[:])
            if store is not None:
                ot, first, cnt = store
                nc.sync.dma_start(out=ov[:, first * RUN * N : (first + cnt) * RUN * N], in_=ot[:])

        for step in range(NCH + 2):
            if step < NCH:
                transposes(step)
                copies(step)
            if 0 <= step - 1 < NCH:
                quantise(step - 1)
            if step - 2 >= 0:
                multiply(step - 2)
